import numpy as np
import ml_dtypes


def mxq(x, axis, fmt="e4m3"):
    dtype, down = {"e4m3": (ml_dtypes.float8_e4m3fn, 7), "e5m2": (ml_dtypes.float8_e5m2, 14)}[fmt]
    v = np.moveaxis(np.asarray(x, np.float32).astype(ml_dtypes.bfloat16).astype(np.float64), axis, -1)
    blocks = v.reshape(v.shape[:-1] + (-1, 32))
    amax = np.abs(blocks).max(-1, keepdims=True)
    byte = np.maximum(np.where(amax > 0, np.frexp(amax)[1] - 1 + 127, 0) - down, 1)
    scale = np.exp2(byte - 127.0)
    codes = (blocks / scale).astype(np.float32).astype(dtype).astype(np.float64)
    return np.moveaxis((codes * scale).reshape(v.shape), -1, axis)


WIDE = False


def mx_kscale(k):
    if not WIDE:
        return np.ones(k)
    levels = np.array([10, -10, 5, -5, 0])
    a = np.random.permutation(np.resize(levels, k // 512 * 4)).reshape(k // 512, 4)
    idx = np.arange(k)
    return np.exp2(a[idx // 512, idx % 128 // 32])


BF16 = ml_dtypes.bfloat16


def bf(x):
    return np.asarray(x, np.float32).astype(BF16)


def f64(x):
    return np.asarray(x).astype(np.float64)


E2M1 = np.array([0.0, 0.5, 1.0, 1.5, 2.0, 3.0, 4.0, 6.0, -0.0, -0.5, -1.0, -1.5, -2.0, -3.0, -4.0, -6.0])


def pack_weight(w, fmt):
    k, n = w.shape
    w = f64(bf(w)).reshape(k // 32, 32, n)
    amax = np.abs(w).max(1)
    if fmt == "e4m3":
        byte = np.frexp(amax)[1] - 1 + 127 - 7
    else:
        mant, ex = np.frexp(amax / 6.0)
        byte = np.where(mant > 0.5, ex, ex - 1) + 127
    byte = np.clip(np.where(amax > 0, byte, 1), 1, 254)
    scaled = (w * np.exp2(127.0 - byte)[:, None, :]).reshape(k, n).astype(np.float32)
    by_word = np.ascontiguousarray(scaled.reshape(k // 512, 128, 4, n).transpose(0, 1, 3, 2))
    if fmt == "e4m3":
        words = by_word.astype(ml_dtypes.float8_e4m3fn).view(np.uint8)
    else:
        c = by_word.astype(ml_dtypes.float4_e2m1fn).view(np.uint8) & 0xF
        words = c[..., 0::2] | (c[..., 1::2] << 4)
    return np.ascontiguousarray(words), np.ascontiguousarray(byte.astype(np.uint8).reshape(k // 512, 16, n))


def unpack_weight(words, scales, fmt):
    g, p, n, _ = words.shape
    if fmt == "e4m3":
        vals = np.ascontiguousarray(words).view(ml_dtypes.float8_e4m3fn).astype(np.float64)
    else:
        nib = np.empty((g, p, n, 4), np.uint8)
        nib[..., 0::2] = words & 0xF
        nib[..., 1::2] = words >> 4
        vals = E2M1[nib]
    vals = vals * np.repeat(np.exp2(scales.astype(np.float64) - 127.0), 8, axis=1)[..., None]
    return vals.transpose(0, 1, 3, 2).reshape(g * 512, n)

def pack4(w):
    words, scales = pack_weight(w, "e2m1")
    return words.reshape(words.shape[0], 128, -1), scales


def unpack4(words, scales):
    return unpack_weight(words.reshape(words.shape[0], 128, -1, 2), scales, "e2m1")


B, N, D1, D2, F1, F2, F3, F4 = 256, 1, 20480, 20480, 128, 64, 32, 16
K = D1 + D2
EPS = 1e-5
SLOPE = 0.2


def setup_inputs():
    s = mx_kscale(K)
    g = np.sqrt(EPS)
    input1 = bf(np.random.standard_normal((B, N, D1)) * s[:D1])
    input2 = bf(np.random.standard_normal((B, N, D2)) * s[D1:])
    w1 = np.random.standard_normal((F1, K)) * 5.0 * g / np.sqrt(K) / s[None, :]
    words, scales = pack4(np.ascontiguousarray(w1.T))
    b1 = bf(np.random.standard_normal(F1) * 2.5 * g)
    return {"input1": input1,
            "input2": input2,
            "W1_words": words,
            "W1_scales": scales,
            "b1": b1}


def reference(input1, input2, W1_words, W1_scales, b1):
    x = np.concatenate([f64(input1), f64(input2)], axis=2)
    h = (mxq(x, 2, "e4m3") @ unpack4(W1_words, W1_scales)) + f64(b1)
    m = h.mean(axis=-1, keepdims=True)
    v = np.square(h - m).mean(axis=-1, keepdims=True)
    hn = (h - m) * (1.0 / np.sqrt(v + EPS))
    return np.where(hn >= 0, hn, SLOPE * hn)

@@ -1,0 +1,217 @@
+from contextlib import ExitStack
+
+import concourse.mybir as mybir
+from concourse.masks import make_identity
+
+F32 = mybir.dt.float32
+BF16 = mybir.dt.bfloat16
+I32 = mybir.dt.int32
+U32 = mybir.dt.uint32
+U8 = mybir.dt.uint8
+FP8X4 = mybir.dt.float8_e4m3fn_x4
+FP4X4 = mybir.dt.float4_e2m1fn_x4
+ALU = mybir.AluOpType
+ACT = mybir.ActivationFunctionType
+
+P = 128
+PACK = 4
+K_GROUP = P * PACK
+ROW_TILES = 2
+D_INPUT = 20480
+GROUPS = 2 * D_INPUT // K_GROUP
+FEATURES = 128
+EPS = 1e-5
+SLOPE = 0.2
+
+ROUND_GROUPS = 8
+ROUND_COLS = ROUND_GROUPS * K_GROUP
+COLUMN_CHUNKS = GROUPS // ROUND_GROUPS
+ROUNDS = COLUMN_CHUNKS * ROW_TILES
+BANK_WORDS = 512
+BANK_GROUPS = BANK_WORDS // (2 * P)
+ROUND_BANKS = ROUND_GROUPS // BANK_GROUPS
+X_BUFFERS = 12
+SCALE_CUTS = 4
+
+FLOPS = 2 * ROW_TILES * P * GROUPS * K_GROUP * FEATURES
+
+
+def tile_fcd_pa_kernel(tc, input1, input2, W1_words, W1_scales, b1, out):
+    nc = tc.nc
+    x_parts = [
+        input1.rearrange("(t p) o k -> t p (o k)", p=P),
+        input2.rearrange("(t p) o k -> t p (o k)", p=P),
+    ]
+    out_tiles = out.rearrange("(t p) o f -> t p (o f)", p=P)
+    words_dram = W1_words.bitcast(I32)
+    scales_dram = W1_scales.bitcast(I32).rearrange("g q n -> q g n")
+
+    with ExitStack() as ctx:
+        keep = ctx.enter_context(tc.tile_pool(name="keep", bufs=1))
+        x_pool = ctx.enter_context(tc.tile_pool(name="x", bufs=X_BUFFERS))
+        stage = ctx.enter_context(tc.tile_pool(name="stage", bufs=3))
+        flip_psum = ctx.enter_context(tc.psum_pool(name="flip", bufs=6))
+        acc_psum = ctx.enter_context(tc.psum_pool(name="acc", bufs=1))
+        ctx.enter_context(tc.manual_schedule())
+
+        w_words = keep.tile([P, GROUPS, 2 * FEATURES], U8, align_bytes=64)
+        w_planes = keep.tile([P, GROUPS, FEATURES], U8, align_bytes=64)
+        identity = keep.tile([P, P], F32)
+        ones = keep.tile([P, P], BF16)
+        bias_row = keep.tile([P, FEATURES], BF16)
+        bias = keep.tile([P, FEATURES], F32)
+        eps = keep.tile([P, 1], F32)
+        warm = keep.tile([P, 1], F32)
+        acc_0 = acc_psum.tile([P, FEATURES], F32)
+        acc_1 = acc_psum.tile([P, FEATURES], F32)
+        acc = [acc_0, acc_1]
+
+        x_tiles = {}
+        flipped = {}
+        grouped_tiles = {}
+        code_tiles = {}
+
+        def load_round(r):
+            chunk, row_tile = divmod(r, ROW_TILES)
+            if row_tile == 0:
+                g0 = chunk * ROUND_GROUPS
+                nc.sync.dma_start(
+                    out=w_words[:, g0 : g0 + ROUND_GROUPS, :].bitcast(I32),
+                    in_=words_dram[g0 : g0 + ROUND_GROUPS].rearrange("g p b -> p g b"),
+                )
+            part, chunk_in_part = divmod(chunk, COLUMN_CHUNKS // 2)
+            c0 = chunk_in_part * ROUND_COLS
+            x_sb = x_pool.tile([P, ROUND_COLS], BF16)
+            nc.sync.dma_start(out=x_sb[:], in_=x_parts[part][row_tile][:, c0 : c0 + ROUND_COLS])
+            x_tiles[r] = x_sb
+
+        def load_scales():
+            cut = GROUPS // SCALE_CUTS
+            for c in range(SCALE_CUTS):
+                for i in range(PACK):
+                    nc.sync.dma_start(
+                        out=w_planes[i:P:32, c * cut : (c + 1) * cut, :].bitcast(I32),
+                        in_=scales_dram[i:16:4, c * cut : (c + 1) * cut, :],
+                    )
+
+        def transpose_round(r):
+            x_words = x_tiles[r][:].bitcast(F32)
+            flipped[r] = []
+            for b in range(ROUND_BANKS):
+                bank = flip_psum.tile([P, 2 * BANK_GROUPS, P], F32, tag="bank")
+                for a in range(BANK_GROUPS):
+                    w0 = (b * BANK_GROUPS + a) * 2 * P
+                    for u in range(2):
+                        nc.tensor.transpose(
+                            bank[:, 2 * a + u, :], x_words[:, w0 + u : w0 + 2 * P : 2], identity[:]
+                        )
+                flipped[r].append(bank)
+
+        def regroup_round(r):
+            grouped = stage.tile([P, ROUND_COLS], BF16, align_bytes=64)
+            grouped_words = grouped[:].bitcast(F32)
+            for b in range(ROUND_BANKS):
+                dst = grouped_words[:, b * BANK_WORDS : (b + 1) * BANK_WORDS].rearrange(
+                    "p (a r u) -> p a r u", a=BANK_GROUPS, u=2
+                )
+                src = flipped[r][b][:].rearrange("p (a u) r -> p a r u", u=2)
+                if b < ROUND_BANKS - 1:
+                    nc.scalar.copy(out=dst, in_=src)
+                else:
+                    nc.vector.tensor_copy(out=dst, in_=src)
+            grouped_tiles[r] = grouped
+
+        def quantise_round(r):
+            codes = stage.tile([P, ROUND_GROUPS * P], U32, align_bytes=64)
+            planes = stage.tile([P, ROUND_GROUPS * P], U8, align_bytes=64)
+            nc.vector.quantize_mx(
+                out=codes[:].bitcast(FP8X4), scales=planes[:], in_=grouped_tiles[r][:]
+            )
+            code_tiles[r] = (codes, planes)
+
+        def multiply_round(r):
+            chunk, row_tile = divmod(r, ROW_TILES)
+            codes, planes = code_tiles[r]
+            for a in range(ROUND_GROUPS):
+                g = chunk * ROUND_GROUPS + a
+                rows = slice(a * P, (a + 1) * P)
+                nc.tensor.matmul_mx(
+                    out=acc[row_tile][:],
+                    lhsT=codes[:, rows].bitcast(FP8X4),
+                    lhsT_scale=planes[:, rows],
+                    rhs=w_words[:, g, :].bitcast(FP4X4),
+                    rhs_scale=w_planes[:, g, :],
+                    start=(g == 0),
+                    stop=(g == GROUPS - 1),
+                )
+
+        h_tiles = {}
+        moment_tiles = {}
+        std_tiles = {}
+
+        def statistics(row_tile):
+            h = keep.tile([P, FEATURES], F32, name="h%d" % row_tile)
+            nc.vector.tensor_tensor(out=h[:], in0=acc[row_tile][:], in1=bias[:], op=ALU.add)
+            stats = keep.tile([P, 6], F32, name="stats%d" % row_tile)
+            nc.vector.bn_stats(out=stats[:], in_=h[:])
+            moments = keep.tile([P, 2], F32, name="moments%d" % row_tile)
+            nc.vector.bn_aggr(out=moments[:], in_=stats[:])
+            std = keep.tile([P, 1], F32, name="std%d" % row_tile)
+            nc.scalar.activation(out=std[:], in_=moments[:, 1:2], func=ACT.Sqrt, bias=eps[:], scale=1.0)
+            h_tiles[row_tile] = h
+            moment_tiles[row_tile] = moments
+            std_tiles[row_tile] = std
+
+        def normalise(row_tile):
+            inv_std = keep.tile([P, 1], F32, name="inv_std%d" % row_tile)
+            nc.vector.reciprocal(out=inv_std[:], in_=std_tiles[row_tile][:])
+            normed = keep.tile([P, FEATURES], F32, name="normed%d" % row_tile)
+            nc.vector.tensor_scalar(
+                out=normed[:],
+                in0=h_tiles[row_tile][:],
+                scalar1=moment_tiles[row_tile][:, 0:1],
+                scalar2=inv_std[:],
+                op0=ALU.subtract,
+                op1=ALU.mult,
+            )
+            result = keep.tile([P, FEATURES], F32, name="result%d" % row_tile)
+            nc.vector.scalar_tensor_tensor(
+                out=result[:], in0=normed[:], scalar=SLOPE, in1=normed[:], op0=ALU.mult, op1=ALU.max
+            )
+            nc.sync.dma_start(out=out_tiles[row_tile], in_=result[:])
+
+        cut = GROUPS // SCALE_CUTS
+        for c in range(SCALE_CUTS):
+            nc.vector.memset(w_planes[:, c * cut : (c + 1) * cut, :].bitcast(I32), 0)
+        nc.vector.memset(eps[:], EPS)
+        nc.gpsimd.memset(bias_row[:], 0.0)
+        nc.gpsimd.memset(ones[:], 1.0)
+        make_identity(nc, identity[:])
+        nc.scalar.dma_start(out=bias_row[0:1, :], in_=b1.unsqueeze(0))
+        nc.scalar.activation(out=warm[:], in_=eps[:], func=ACT.Sqrt)
+
+        load_round(0)
+        load_scales()
+        for r in range(1, X_BUFFERS):
+            load_round(r)
+
+        bias_bank = flip_psum.tile([P, 2 * BANK_GROUPS, P], F32, tag="bank")
+        nc.tensor.matmul(out=bias_bank[:, 0, :], lhsT=ones[:], rhs=bias_row[:], start=True, stop=True)
+        nc.vector.tensor_copy(out=bias[:], in_=bias_bank[:, 0, :])
+
+        for r in range(ROUNDS + 1):
+            if r < ROUNDS:
+                transpose_round(r)
+            if r >= 1:
+                quantise_round(r - 1)
+            if r < ROUNDS:
+                regroup_round(r)
+                if r + X_BUFFERS < ROUNDS:
+                    load_round(r + X_BUFFERS)
+            if r >= 1:
+                multiply_round(r - 1)
+
+        statistics(0)
+        statistics(1)
+        normalise(0)
+        normalise(1)

@@ -30,7 +30,7 @@ ROUNDS = COLUMN_CHUNKS * ROW_TILES
 BANK_WORDS = 512
 BANK_GROUPS = BANK_WORDS // (2 * P)
 ROUND_BANKS = ROUND_GROUPS // BANK_GROUPS
-X_BUFFERS = 12
+X_BUFFERS = 8
 SCALE_CUTS = 4
 
 FLOPS = 2 * ROW_TILES * P * GROUPS * K_GROUP * FEATURES
@@ -67,6 +67,7 @@ def tile_fcd_pa_kernel(tc, input1, input2, W1_words, W1_scales, b1, out):
         acc = [acc_0, acc_1]
 
         x_tiles = {}
+        sorted_tiles = {}
         flipped = {}
         grouped_tiles = {}
         code_tiles = {}
@@ -94,17 +95,22 @@ def tile_fcd_pa_kernel(tc, input1, input2, W1_words, W1_scales, b1, out):
                         in_=scales_dram[i:16:4, c * cut : (c + 1) * cut, :],
                     )
 
+        def sort_round(r):
+            sorted_words = stage.tile([P, ROUND_COLS // 2], F32)
+            nc.vector.tensor_copy(
+                out=sorted_words[:].rearrange("p (g u q) -> p g u q", g=ROUND_GROUPS, u=2),
+                in_=x_tiles[r][:].bitcast(F32).rearrange("p (g q u) -> p g u q", g=ROUND_GROUPS, u=2),
+            )
+            sorted_tiles[r] = sorted_words
+
         def transpose_round(r):
-            x_words = x_tiles[r][:].bitcast(F32)
+            sorted_words = sorted_tiles[r]
             flipped[r] = []
             for b in range(ROUND_BANKS):
                 bank = flip_psum.tile([P, 2 * BANK_GROUPS, P], F32, tag="bank")
-                for a in range(BANK_GROUPS):
-                    w0 = (b * BANK_GROUPS + a) * 2 * P
-                    for u in range(2):
-                        nc.tensor.transpose(
-                            bank[:, 2 * a + u, :], x_words[:, w0 + u : w0 + 2 * P : 2], identity[:]
-                        )
+                for i in range(2 * BANK_GROUPS):
+                    w0 = (b * 2 * BANK_GROUPS + i) * P
+                    nc.tensor.transpose(bank[:, i, :], sorted_words[:, w0 : w0 + P], identity[:])
                 flipped[r].append(bank)
 
         def regroup_round(r):
@@ -115,10 +121,7 @@ def tile_fcd_pa_kernel(tc, input1, input2, W1_words, W1_scales, b1, out):
                     "p (a r u) -> p a r u", a=BANK_GROUPS, u=2
                 )
                 src = flipped[r][b][:].rearrange("p (a u) r -> p a r u", u=2)
-                if b < ROUND_BANKS - 1:
-                    nc.scalar.copy(out=dst, in_=src)
-                else:
-                    nc.vector.tensor_copy(out=dst, in_=src)
+                nc.scalar.copy(out=dst, in_=src)
             grouped_tiles[r] = grouped
 
         def quantise_round(r):
@@ -201,6 +204,7 @@ def tile_fcd_pa_kernel(tc, input1, input2, W1_words, W1_scales, b1, out):
 
         for r in range(ROUNDS + 1):
             if r < ROUNDS:
+                sort_round(r)
                 transpose_round(r)
             if r >= 1:
                 quantise_round(r - 1)

@@ -30,8 +30,13 @@ ROUNDS = COLUMN_CHUNKS * ROW_TILES
 BANK_WORDS = 512
 BANK_GROUPS = BANK_WORDS // (2 * P)
 ROUND_BANKS = ROUND_GROUPS // BANK_GROUPS
-X_BUFFERS = 8
-SCALE_CUTS = 4
+BANK_COLS = BANK_GROUPS * K_GROUP
+SORTED_BANK = ROUND_BANKS - 1
+X_BUFFERS = 12
+SCALE_CUTS = 5
+CUT_GROUPS = GROUPS // SCALE_CUTS
+CUT_ROUNDS = ROUNDS // SCALE_CUTS
+SCALE_LEAD = 2
 
 FLOPS = 2 * ROW_TILES * P * GROUPS * K_GROUP * FEATURES
 
@@ -74,7 +79,9 @@ def tile_fcd_pa_kernel(tc, input1, input2, W1_words, W1_scales, b1, out):
 
         def load_round(r):
             chunk, row_tile = divmod(r, ROW_TILES)
-            if row_tile == 0:
+            if (r + SCALE_LEAD) % CUT_ROUNDS == 0 and r + SCALE_LEAD < ROUNDS:
+                load_scales((r + SCALE_LEAD) // CUT_ROUNDS)
+            if row_tile == 1:
                 g0 = chunk * ROUND_GROUPS
                 nc.sync.dma_start(
                     out=w_words[:, g0 : g0 + ROUND_GROUPS, :].bitcast(I32),
@@ -83,59 +90,81 @@ def tile_fcd_pa_kernel(tc, input1, input2, W1_words, W1_scales, b1, out):
             part, chunk_in_part = divmod(chunk, COLUMN_CHUNKS // 2)
             c0 = chunk_in_part * ROUND_COLS
             x_sb = x_pool.tile([P, ROUND_COLS], BF16)
-            nc.sync.dma_start(out=x_sb[:], in_=x_parts[part][row_tile][:, c0 : c0 + ROUND_COLS])
+            pieces = ROUND_BANKS if r == ROUNDS - 1 else 1
+            width = ROUND_COLS // pieces
+            for i in range(pieces):
+                nc.sync.dma_start(
+                    out=x_sb[:, i * width : (i + 1) * width],
+                    in_=x_parts[part][row_tile][:, c0 + i * width : c0 + (i + 1) * width],
+                )
             x_tiles[r] = x_sb
 
-        def load_scales():
-            cut = GROUPS // SCALE_CUTS
-            for c in range(SCALE_CUTS):
-                for i in range(PACK):
-                    nc.sync.dma_start(
-                        out=w_planes[i:P:32, c * cut : (c + 1) * cut, :].bitcast(I32),
-                        in_=scales_dram[i:16:4, c * cut : (c + 1) * cut, :],
-                    )
+        def load_scales(c):
+            groups = slice(c * CUT_GROUPS, (c + 1) * CUT_GROUPS)
+            for i in range(PACK):
+                nc.sync.dma_start(
+                    out=w_planes[i:P:32, groups, :].bitcast(I32), in_=scales_dram[i:16:4, groups, :]
+                )
 
         def sort_round(r):
-            sorted_words = stage.tile([P, ROUND_COLS // 2], F32)
-            nc.vector.tensor_copy(
-                out=sorted_words[:].rearrange("p (g u q) -> p g u q", g=ROUND_GROUPS, u=2),
-                in_=x_tiles[r][:].bitcast(F32).rearrange("p (g q u) -> p g u q", g=ROUND_GROUPS, u=2),
+            x_words = x_tiles[r][:].bitcast(F32)
+            sorted_words = stage.tile([P, BANK_WORDS], F32)
+            nc.scalar.copy(
+                out=sorted_words[:].rearrange("p (a u q) -> p a u q", a=BANK_GROUPS, u=2),
+                in_=x_words[:, SORTED_BANK * BANK_WORDS : (SORTED_BANK + 1) * BANK_WORDS].rearrange(
+                    "p (a q u) -> p a u q", a=BANK_GROUPS, u=2
+                ),
             )
             sorted_tiles[r] = sorted_words
 
         def transpose_round(r):
-            sorted_words = sorted_tiles[r]
+            x_words = x_tiles[r][:].bitcast(F32)
             flipped[r] = []
             for b in range(ROUND_BANKS):
                 bank = flip_psum.tile([P, 2 * BANK_GROUPS, P], F32, tag="bank")
-                for i in range(2 * BANK_GROUPS):
-                    w0 = (b * 2 * BANK_GROUPS + i) * P
-                    nc.tensor.transpose(bank[:, i, :], sorted_words[:, w0 : w0 + P], identity[:])
+                for a in range(BANK_GROUPS):
+                    for u in range(2):
+                        if b == SORTED_BANK:
+                            w0 = (2 * a + u) * P
+                            run = sorted_tiles[r][:, w0 : w0 + P]
+                        else:
+                            w0 = (b * BANK_GROUPS + a) * 2 * P
+                            run = x_words[:, w0 + u : w0 + 2 * P : 2]
+                        nc.tensor.transpose(bank[:, 2 * a + u, :], run, identity[:])
                 flipped[r].append(bank)
 
-        def regroup_round(r):
+        def open_round(r):
             grouped = stage.tile([P, ROUND_COLS], BF16, align_bytes=64)
-            grouped_words = grouped[:].bitcast(F32)
-            for b in range(ROUND_BANKS):
-                dst = grouped_words[:, b * BANK_WORDS : (b + 1) * BANK_WORDS].rearrange(
-                    "p (a r u) -> p a r u", a=BANK_GROUPS, u=2
-                )
-                src = flipped[r][b][:].rearrange("p (a u) r -> p a r u", u=2)
-                nc.scalar.copy(out=dst, in_=src)
-            grouped_tiles[r] = grouped
-
-        def quantise_round(r):
             codes = stage.tile([P, ROUND_GROUPS * P], U32, align_bytes=64)
             planes = stage.tile([P, ROUND_GROUPS * P], U8, align_bytes=64)
-            nc.vector.quantize_mx(
-                out=codes[:].bitcast(FP8X4), scales=planes[:], in_=grouped_tiles[r][:]
-            )
+            grouped_tiles[r] = grouped
             code_tiles[r] = (codes, planes)
 
-        def multiply_round(r):
+        def regroup_bank(r, b):
+            dst = (
+                grouped_tiles[r][:]
+                .bitcast(F32)[:, b * BANK_WORDS : (b + 1) * BANK_WORDS]
+                .rearrange("p (a r u) -> p a r u", a=BANK_GROUPS, u=2)
+            )
+            src = flipped[r][b][:].rearrange("p (a u) r -> p a r u", u=2)
+            if b < ROUND_BANKS - 1:
+                nc.scalar.copy(out=dst, in_=src)
+            else:
+                nc.vector.tensor_copy(out=dst, in_=src)
+
+        def quantise_banks(r, b0, n_banks):
+            codes, planes = code_tiles[r]
+            words = slice(b0 * BANK_COLS // PACK, (b0 + n_banks) * BANK_COLS // PACK)
+            nc.vector.quantize_mx(
+                out=codes[:, words].bitcast(FP8X4),
+                scales=planes[:, words],
+                in_=grouped_tiles[r][:, b0 * BANK_COLS : (b0 + n_banks) * BANK_COLS],
+            )
+
+        def multiply_banks(r, b0, n_banks):
             chunk, row_tile = divmod(r, ROW_TILES)
             codes, planes = code_tiles[r]
-            for a in range(ROUND_GROUPS):
+            for a in range(b0 * BANK_GROUPS, (b0 + n_banks) * BANK_GROUPS):
                 g = chunk * ROUND_GROUPS + a
                 rows = slice(a * P, (a + 1) * P)
                 nc.tensor.matmul_mx(
@@ -183,9 +212,8 @@ def tile_fcd_pa_kernel(tc, input1, input2, W1_words, W1_scales, b1, out):
             )
             nc.sync.dma_start(out=out_tiles[row_tile], in_=result[:])
 
-        cut = GROUPS // SCALE_CUTS
         for c in range(SCALE_CUTS):
-            nc.vector.memset(w_planes[:, c * cut : (c + 1) * cut, :].bitcast(I32), 0)
+            nc.vector.memset(w_planes[:, c * CUT_GROUPS : (c + 1) * CUT_GROUPS, :].bitcast(I32), 0)
         nc.vector.memset(eps[:], EPS)
         nc.gpsimd.memset(bias_row[:], 0.0)
         nc.gpsimd.memset(ones[:], 1.0)
@@ -194,7 +222,7 @@ def tile_fcd_pa_kernel(tc, input1, input2, W1_words, W1_scales, b1, out):
         nc.scalar.activation(out=warm[:], in_=eps[:], func=ACT.Sqrt)
 
         load_round(0)
-        load_scales()
+        load_scales(0)
         for r in range(1, X_BUFFERS):
             load_round(r)
 
@@ -202,18 +230,23 @@ def tile_fcd_pa_kernel(tc, input1, input2, W1_words, W1_scales, b1, out):
         nc.tensor.matmul(out=bias_bank[:, 0, :], lhsT=ones[:], rhs=bias_row[:], start=True, stop=True)
         nc.vector.tensor_copy(out=bias[:], in_=bias_bank[:, 0, :])
 
-        for r in range(ROUNDS + 1):
-            if r < ROUNDS:
-                sort_round(r)
-                transpose_round(r)
+        last = ROUNDS - 1
+        for r in range(ROUNDS):
+            open_round(r)
+            sort_round(r)
+            transpose_round(r)
             if r >= 1:
-                quantise_round(r - 1)
-            if r < ROUNDS:
-                regroup_round(r)
-                if r + X_BUFFERS < ROUNDS:
-                    load_round(r + X_BUFFERS)
+                quantise_banks(r - 1, 0, ROUND_BANKS)
+            for b in range(ROUND_BANKS):
+                regroup_bank(r, b)
+                if r == last:
+                    quantise_banks(r, b, 1)
+            if r + X_BUFFERS < ROUNDS:
+                load_round(r + X_BUFFERS)
             if r >= 1:
-                multiply_round(r - 1)
+                multiply_banks(r - 1, 0, ROUND_BANKS)
+        for b in range(ROUND_BANKS):
+            multiply_banks(last, b, 1)
 
         statistics(0)
         statistics(1)

@@ -31,7 +31,9 @@ BANK_WORDS = 512
 BANK_GROUPS = BANK_WORDS // (2 * P)
 ROUND_BANKS = ROUND_GROUPS // BANK_GROUPS
 BANK_COLS = BANK_GROUPS * K_GROUP
-SORTED_BANK = ROUND_BANKS - 1
+SORTED_BANKS = 2
+FIRST_SORTED = ROUND_BANKS - SORTED_BANKS
+HALF_BANKS = ROUND_BANKS // 2
 X_BUFFERS = 12
 SCALE_CUTS = 5
 CUT_GROUPS = GROUPS // SCALE_CUTS
@@ -108,11 +110,11 @@ def tile_fcd_pa_kernel(tc, input1, input2, W1_words, W1_scales, b1, out):
 
         def sort_round(r):
             x_words = x_tiles[r][:].bitcast(F32)
-            sorted_words = stage.tile([P, BANK_WORDS], F32)
-            nc.scalar.copy(
-                out=sorted_words[:].rearrange("p (a u q) -> p a u q", a=BANK_GROUPS, u=2),
-                in_=x_words[:, SORTED_BANK * BANK_WORDS : (SORTED_BANK + 1) * BANK_WORDS].rearrange(
-                    "p (a q u) -> p a u q", a=BANK_GROUPS, u=2
+            sorted_words = stage.tile([P, SORTED_BANKS * BANK_WORDS], F32)
+            nc.vector.tensor_copy(
+                out=sorted_words[:].rearrange("p (a u q) -> p a u q", a=SORTED_BANKS * BANK_GROUPS, u=2),
+                in_=x_words[:, FIRST_SORTED * BANK_WORDS :].rearrange(
+                    "p (a q u) -> p a u q", a=SORTED_BANKS * BANK_GROUPS, u=2
                 ),
             )
             sorted_tiles[r] = sorted_words
@@ -124,8 +126,8 @@ def tile_fcd_pa_kernel(tc, input1, input2, W1_words, W1_scales, b1, out):
                 bank = flip_psum.tile([P, 2 * BANK_GROUPS, P], F32, tag="bank")
                 for a in range(BANK_GROUPS):
                     for u in range(2):
-                        if b == SORTED_BANK:
-                            w0 = (2 * a + u) * P
+                        if b >= FIRST_SORTED:
+                            w0 = (2 * ((b - FIRST_SORTED) * BANK_GROUPS + a) + u) * P
                             run = sorted_tiles[r][:, w0 : w0 + P]
                         else:
                             w0 = (b * BANK_GROUPS + a) * 2 * P
@@ -147,10 +149,7 @@ def tile_fcd_pa_kernel(tc, input1, input2, W1_words, W1_scales, b1, out):
                 .rearrange("p (a r u) -> p a r u", a=BANK_GROUPS, u=2)
             )
             src = flipped[r][b][:].rearrange("p (a u) r -> p a r u", u=2)
-            if b < ROUND_BANKS - 1:
-                nc.scalar.copy(out=dst, in_=src)
-            else:
-                nc.vector.tensor_copy(out=dst, in_=src)
+            nc.scalar.copy(out=dst, in_=src)
 
         def quantise_banks(r, b0, n_banks):
             codes, planes = code_tiles[r]
@@ -231,16 +230,20 @@ def tile_fcd_pa_kernel(tc, input1, input2, W1_words, W1_scales, b1, out):
         nc.vector.tensor_copy(out=bias[:], in_=bias_bank[:, 0, :])
 
         last = ROUNDS - 1
+        sort_round(0)
         for r in range(ROUNDS):
             open_round(r)
-            sort_round(r)
             transpose_round(r)
             if r >= 1:
-                quantise_banks(r - 1, 0, ROUND_BANKS)
+                quantise_banks(r - 1, HALF_BANKS, HALF_BANKS)
+            if r < last:
+                sort_round(r + 1)
             for b in range(ROUND_BANKS):
                 regroup_bank(r, b)
                 if r == last:
                     quantise_banks(r, b, 1)
+                elif b == HALF_BANKS - 1:
+                    quantise_banks(r, 0, HALF_BANKS)
             if r + X_BUFFERS < ROUNDS:
                 load_round(r + X_BUFFERS)
             if r >= 1:

@@ -37,8 +37,6 @@ HALF_BANKS = ROUND_BANKS // 2
 X_BUFFERS = 12
 SCALE_CUTS = 5
 CUT_GROUPS = GROUPS // SCALE_CUTS
-CUT_ROUNDS = ROUNDS // SCALE_CUTS
-SCALE_LEAD = 2
 
 FLOPS = 2 * ROW_TILES * P * GROUPS * K_GROUP * FEATURES
 
@@ -51,7 +49,7 @@ def tile_fcd_pa_kernel(tc, input1, input2, W1_words, W1_scales, b1, out):
     ]
     out_tiles = out.rearrange("(t p) o f -> t p (o f)", p=P)
     words_dram = W1_words.bitcast(I32)
-    scales_dram = W1_scales.bitcast(I32).rearrange("g q n -> q g n")
+    scale_views = {dt: W1_scales.bitcast(dt).rearrange("g q n -> q g n") for dt in (I32, F32)}
 
     with ExitStack() as ctx:
         keep = ctx.enter_context(tc.tile_pool(name="keep", bufs=1))
@@ -81,8 +79,6 @@ def tile_fcd_pa_kernel(tc, input1, input2, W1_words, W1_scales, b1, out):
 
         def load_round(r):
             chunk, row_tile = divmod(r, ROW_TILES)
-            if (r + SCALE_LEAD) % CUT_ROUNDS == 0 and r + SCALE_LEAD < ROUNDS:
-                load_scales((r + SCALE_LEAD) // CUT_ROUNDS)
             if row_tile == 1:
                 g0 = chunk * ROUND_GROUPS
                 nc.sync.dma_start(
@@ -101,11 +97,11 @@ def tile_fcd_pa_kernel(tc, input1, input2, W1_words, W1_scales, b1, out):
                 )
             x_tiles[r] = x_sb
 
-        def load_scales(c):
+        def load_scales(c, queue, dt):
             groups = slice(c * CUT_GROUPS, (c + 1) * CUT_GROUPS)
             for i in range(PACK):
-                nc.sync.dma_start(
-                    out=w_planes[i:P:32, groups, :].bitcast(I32), in_=scales_dram[i:16:4, groups, :]
+                queue.dma_start(
+                    out=w_planes[i:P:32, groups, :].bitcast(dt), in_=scale_views[dt][i:16:4, groups, :]
                 )
 
         def sort_round(r):
@@ -126,7 +122,7 @@ def tile_fcd_pa_kernel(tc, input1, input2, W1_words, W1_scales, b1, out):
                 bank = flip_psum.tile([P, 2 * BANK_GROUPS, P], F32, tag="bank")
                 for a in range(BANK_GROUPS):
                     for u in range(2):
-                        if b >= FIRST_SORTED:
+                        if b >= FIRST_SORTED and r in sorted_tiles:
                             w0 = (2 * ((b - FIRST_SORTED) * BANK_GROUPS + a) + u) * P
                             run = sorted_tiles[r][:, w0 : w0 + P]
                         else:
@@ -221,7 +217,9 @@ def tile_fcd_pa_kernel(tc, input1, input2, W1_words, W1_scales, b1, out):
         nc.scalar.activation(out=warm[:], in_=eps[:], func=ACT.Sqrt)
 
         load_round(0)
-        load_scales(0)
+        load_scales(0, nc.sync, I32)
+        for c in range(1, SCALE_CUTS):
+            load_scales(c, nc.gpsimd, F32)
         for r in range(1, X_BUFFERS):
             load_round(r)
 
@@ -236,7 +234,7 @@ def tile_fcd_pa_kernel(tc, input1, input2, W1_words, W1_scales, b1, out):
             transpose_round(r)
             if r >= 1:
                 quantise_banks(r - 1, HALF_BANKS, HALF_BANKS)
-            if r < last:
+            if r + 1 < last:
                 sort_round(r + 1)
             for b in range(ROUND_BANKS):
                 regroup_bank(r, b)

@@ -35,6 +35,8 @@ SORTED_BANKS = 2
 FIRST_SORTED = ROUND_BANKS - SORTED_BANKS
 HALF_BANKS = ROUND_BANKS // 2
 X_BUFFERS = 12
+LATE_CHUNKS = 2
+FIRST_LATE = ROUNDS - LATE_CHUNKS * ROW_TILES
 SCALE_CUTS = 5
 CUT_GROUPS = GROUPS // SCALE_CUTS
 
@@ -55,6 +57,7 @@ def tile_fcd_pa_kernel(tc, input1, input2, W1_words, W1_scales, b1, out):
         keep = ctx.enter_context(tc.tile_pool(name="keep", bufs=1))
         x_pool = ctx.enter_context(tc.tile_pool(name="x", bufs=X_BUFFERS))
         stage = ctx.enter_context(tc.tile_pool(name="stage", bufs=3))
+        code_pool = ctx.enter_context(tc.tile_pool(name="codes", bufs=LATE_CHUNKS * ROW_TILES + 1))
         flip_psum = ctx.enter_context(tc.psum_pool(name="flip", bufs=6))
         acc_psum = ctx.enter_context(tc.psum_pool(name="acc", bufs=1))
         ctx.enter_context(tc.manual_schedule())
@@ -77,25 +80,25 @@ def tile_fcd_pa_kernel(tc, input1, input2, W1_words, W1_scales, b1, out):
         grouped_tiles = {}
         code_tiles = {}
 
+        def load_words(chunk):
+            g0 = chunk * ROUND_GROUPS
+            nc.sync.dma_start(
+                out=w_words[:, g0 : g0 + ROUND_GROUPS, :].bitcast(I32),
+                in_=words_dram[g0 : g0 + ROUND_GROUPS].rearrange("g p b -> p g b"),
+            )
+
         def load_round(r):
             chunk, row_tile = divmod(r, ROW_TILES)
-            if row_tile == 1:
-                g0 = chunk * ROUND_GROUPS
-                nc.sync.dma_start(
-                    out=w_words[:, g0 : g0 + ROUND_GROUPS, :].bitcast(I32),
-                    in_=words_dram[g0 : g0 + ROUND_GROUPS].rearrange("g p b -> p g b"),
-                )
+            if row_tile == 1 and r < FIRST_LATE:
+                load_words(chunk)
             part, chunk_in_part = divmod(chunk, COLUMN_CHUNKS // 2)
             c0 = chunk_in_part * ROUND_COLS
             x_sb = x_pool.tile([P, ROUND_COLS], BF16)
-            pieces = ROUND_BANKS if r == ROUNDS - 1 else 1
-            width = ROUND_COLS // pieces
-            for i in range(pieces):
-                nc.sync.dma_start(
-                    out=x_sb[:, i * width : (i + 1) * width],
-                    in_=x_parts[part][row_tile][:, c0 + i * width : c0 + (i + 1) * width],
-                )
+            nc.sync.dma_start(out=x_sb[:], in_=x_parts[part][row_tile][:, c0 : c0 + ROUND_COLS])
             x_tiles[r] = x_sb
+            if r == ROUNDS - 1:
+                for late in range(COLUMN_CHUNKS - LATE_CHUNKS, COLUMN_CHUNKS):
+                    load_words(late)
 
         def load_scales(c, queue, dt):
             groups = slice(c * CUT_GROUPS, (c + 1) * CUT_GROUPS)
@@ -122,7 +125,7 @@ def tile_fcd_pa_kernel(tc, input1, input2, W1_words, W1_scales, b1, out):
                 bank = flip_psum.tile([P, 2 * BANK_GROUPS, P], F32, tag="bank")
                 for a in range(BANK_GROUPS):
                     for u in range(2):
-                        if b >= FIRST_SORTED and r in sorted_tiles:
+                        if b >= FIRST_SORTED:
                             w0 = (2 * ((b - FIRST_SORTED) * BANK_GROUPS + a) + u) * P
                             run = sorted_tiles[r][:, w0 : w0 + P]
                         else:
@@ -133,8 +136,8 @@ def tile_fcd_pa_kernel(tc, input1, input2, W1_words, W1_scales, b1, out):
 
         def open_round(r):
             grouped = stage.tile([P, ROUND_COLS], BF16, align_bytes=64)
-            codes = stage.tile([P, ROUND_GROUPS * P], U32, align_bytes=64)
-            planes = stage.tile([P, ROUND_GROUPS * P], U8, align_bytes=64)
+            codes = code_pool.tile([P, ROUND_GROUPS * P], U32, align_bytes=64)
+            planes = code_pool.tile([P, ROUND_GROUPS * P], U8, align_bytes=64)
             grouped_tiles[r] = grouped
             code_tiles[r] = (codes, planes)
 
@@ -184,14 +187,15 @@ def tile_fcd_pa_kernel(tc, input1, input2, W1_words, W1_scales, b1, out):
             moments = keep.tile([P, 2], F32, name="moments%d" % row_tile)
             nc.vector.bn_aggr(out=moments[:], in_=stats[:])
             std = keep.tile([P, 1], F32, name="std%d" % row_tile)
-            nc.scalar.activation(out=std[:], in_=moments[:, 1:2], func=ACT.Sqrt, bias=eps[:], scale=1.0)
+            nc.scalar.activation(
+                out=std[:], in_=moments[:, 1:2], func=ACT.Abs_reciprocal_sqrt, bias=eps[:], scale=1.0
+            )
             h_tiles[row_tile] = h
             moment_tiles[row_tile] = moments
             std_tiles[row_tile] = std
 
         def normalise(row_tile):
-            inv_std = keep.tile([P, 1], F32, name="inv_std%d" % row_tile)
-            nc.vector.reciprocal(out=inv_std[:], in_=std_tiles[row_tile][:])
+            inv_std = std_tiles[row_tile]
             normed = keep.tile([P, FEATURES], F32, name="normed%d" % row_tile)
             nc.vector.tensor_scalar(
                 out=normed[:],
@@ -214,7 +218,7 @@ def tile_fcd_pa_kernel(tc, input1, input2, W1_words, W1_scales, b1, out):
         nc.gpsimd.memset(ones[:], 1.0)
         make_identity(nc, identity[:])
         nc.scalar.dma_start(out=bias_row[0:1, :], in_=b1.unsqueeze(0))
-        nc.scalar.activation(out=warm[:], in_=eps[:], func=ACT.Sqrt)
+        nc.scalar.activation(out=warm[:], in_=eps[:], func=ACT.Abs_reciprocal_sqrt)
 
         load_round(0)
         load_scales(0, nc.sync, I32)
@@ -234,22 +238,21 @@ def tile_fcd_pa_kernel(tc, input1, input2, W1_words, W1_scales, b1, out):
             transpose_round(r)
             if r >= 1:
                 quantise_banks(r - 1, HALF_BANKS, HALF_BANKS)
-            if r + 1 < last:
+            if r < last:
                 sort_round(r + 1)
             for b in range(ROUND_BANKS):
                 regroup_bank(r, b)
-                if r == last:
-                    quantise_banks(r, b, 1)
-                elif b == HALF_BANKS - 1:
+                if b == HALF_BANKS - 1:
                     quantise_banks(r, 0, HALF_BANKS)
             if r + X_BUFFERS < ROUNDS:
                 load_round(r + X_BUFFERS)
-            if r >= 1:
+            if 1 <= r <= FIRST_LATE:
                 multiply_banks(r - 1, 0, ROUND_BANKS)
-        for b in range(ROUND_BANKS):
-            multiply_banks(last, b, 1)
+        quantise_banks(last, HALF_BANKS, HALF_BANKS)
 
-        statistics(0)
-        statistics(1)
+        for row_tile in range(ROW_TILES):
+            for r in range(FIRST_LATE + row_tile, ROUNDS, ROW_TILES):
+                multiply_banks(r, 0, ROUND_BANKS)
+            statistics(row_tile)
         normalise(0)
         normalise(1)

@@ -35,7 +35,7 @@ SORTED_BANKS = 2
 FIRST_SORTED = ROUND_BANKS - SORTED_BANKS
 HALF_BANKS = ROUND_BANKS // 2
 X_BUFFERS = 12
-LATE_CHUNKS = 2
+LATE_CHUNKS = 3
 FIRST_LATE = ROUNDS - LATE_CHUNKS * ROW_TILES
 SCALE_CUTS = 5
 CUT_GROUPS = GROUPS // SCALE_CUTS
@@ -250,9 +250,9 @@ def tile_fcd_pa_kernel(tc, input1, input2, W1_words, W1_scales, b1, out):
                 multiply_banks(r - 1, 0, ROUND_BANKS)
         quantise_banks(last, HALF_BANKS, HALF_BANKS)
 
-        for row_tile in range(ROW_TILES):
-            for r in range(FIRST_LATE + row_tile, ROUNDS, ROW_TILES):
-                multiply_banks(r, 0, ROUND_BANKS)
-            statistics(row_tile)
+        for r in range(FIRST_LATE, ROUNDS):
+            multiply_banks(r, 0, ROUND_BANKS)
+            if r >= ROUNDS - ROW_TILES:
+                statistics(r - (ROUNDS - ROW_TILES))
         normalise(0)
         normalise(1)

from contextlib import ExitStack

import concourse.mybir as mybir
from concourse.masks import make_identity

F32 = mybir.dt.float32
BF16 = mybir.dt.bfloat16
I32 = mybir.dt.int32
U32 = mybir.dt.uint32
U8 = mybir.dt.uint8
FP8X4 = mybir.dt.float8_e4m3fn_x4
FP4X4 = mybir.dt.float4_e2m1fn_x4
ALU = mybir.AluOpType
ACT = mybir.ActivationFunctionType

P = 128
PACK = 4
K_GROUP = P * PACK
ROW_TILES = 2
D_INPUT = 20480
GROUPS = 2 * D_INPUT // K_GROUP
FEATURES = 128
EPS = 1e-5
SLOPE = 0.2

ROUND_GROUPS = 8
ROUND_COLS = ROUND_GROUPS * K_GROUP
COLUMN_CHUNKS = GROUPS // ROUND_GROUPS
ROUNDS = COLUMN_CHUNKS * ROW_TILES
BANK_WORDS = 512
BANK_GROUPS = BANK_WORDS // (2 * P)
ROUND_BANKS = ROUND_GROUPS // BANK_GROUPS
BANK_COLS = BANK_GROUPS * K_GROUP
SORTED_BANKS = 2
FIRST_SORTED = ROUND_BANKS - SORTED_BANKS
HALF_BANKS = ROUND_BANKS // 2
X_BUFFERS = 12
LATE_CHUNKS = 3
FIRST_LATE = ROUNDS - LATE_CHUNKS * ROW_TILES
SCALE_CUTS = 5
CUT_GROUPS = GROUPS // SCALE_CUTS

FLOPS = 2 * ROW_TILES * P * GROUPS * K_GROUP * FEATURES


def tile_fcd_pa_kernel(tc, input1, input2, W1_words, W1_scales, b1, out):
    nc = tc.nc
    x_parts = [
        input1.rearrange("(t p) o k -> t p (o k)", p=P),
        input2.rearrange("(t p) o k -> t p (o k)", p=P),
    ]
    out_tiles = out.rearrange("(t p) o f -> t p (o f)", p=P)
    words_dram = W1_words.bitcast(I32)
    scale_views = {dt: W1_scales.bitcast(dt).rearrange("g q n -> q g n") for dt in (I32, F32)}

    with ExitStack() as ctx:
        keep = ctx.enter_context(tc.tile_pool(name="keep", bufs=1))
        x_pool = ctx.enter_context(tc.tile_pool(name="x", bufs=X_BUFFERS))
        stage = ctx.enter_context(tc.tile_pool(name="stage", bufs=3))
        code_pool = ctx.enter_context(tc.tile_pool(name="codes", bufs=LATE_CHUNKS * ROW_TILES + 1))
        flip_psum = ctx.enter_context(tc.psum_pool(name="flip", bufs=6))
        acc_psum = ctx.enter_context(tc.psum_pool(name="acc", bufs=1))
        ctx.enter_context(tc.manual_schedule())

        w_words = keep.tile([P, GROUPS, 2 * FEATURES], U8, align_bytes=64)
        w_planes = keep.tile([P, GROUPS, FEATURES], U8, align_bytes=64)
        identity = keep.tile([P, P], F32)
        ones = keep.tile([P, P], BF16)
        bias_row = keep.tile([P, FEATURES], BF16)
        bias = keep.tile([P, FEATURES], F32)
        eps = keep.tile([P, 1], F32)
        warm = keep.tile([P, 1], F32)
        acc_0 = acc_psum.tile([P, FEATURES], F32)
        acc_1 = acc_psum.tile([P, FEATURES], F32)
        acc = [acc_0, acc_1]

        x_tiles = {}
        sorted_tiles = {}
        flipped = {}
        grouped_tiles = {}
        code_tiles = {}

        def load_words(chunk):
            g0 = chunk * ROUND_GROUPS
            nc.sync.dma_start(
                out=w_words[:, g0 : g0 + ROUND_GROUPS, :].bitcast(I32),
                in_=words_dram[g0 : g0 + ROUND_GROUPS].rearrange("g p b -> p g b"),
            )

        def load_round(r):
            chunk, row_tile = divmod(r, ROW_TILES)
            if row_tile == 1 and r < FIRST_LATE:
                load_words(chunk)
            part, chunk_in_part = divmod(chunk, COLUMN_CHUNKS // 2)
            c0 = chunk_in_part * ROUND_COLS
            x_sb = x_pool.tile([P, ROUND_COLS], BF16)
            nc.sync.dma_start(out=x_sb[:], in_=x_parts[part][row_tile][:, c0 : c0 + ROUND_COLS])
            x_tiles[r] = x_sb
            if r == ROUNDS - 1:
                for late in range(COLUMN_CHUNKS - LATE_CHUNKS, COLUMN_CHUNKS):
                    load_words(late)

        def load_scales(c, queue, dt):
            groups = slice(c * CUT_GROUPS, (c + 1) * CUT_GROUPS)
            for i in range(PACK):
                queue.dma_start(
                    out=w_planes[i:P:32, groups, :].bitcast(dt), in_=scale_views[dt][i:16:4, groups, :]
                )

        def sort_round(r):
            x_words = x_tiles[r][:].bitcast(F32)
            sorted_words = stage.tile([P, SORTED_BANKS * BANK_WORDS], F32)
            nc.vector.tensor_copy(
                out=sorted_words[:].rearrange("p (a u q) -> p a u q", a=SORTED_BANKS * BANK_GROUPS, u=2),
                in_=x_words[:, FIRST_SORTED * BANK_WORDS :].rearrange(
                    "p (a q u) -> p a u q", a=SORTED_BANKS * BANK_GROUPS, u=2
                ),
            )
            sorted_tiles[r] = sorted_words

        def transpose_round(r):
            x_words = x_tiles[r][:].bitcast(F32)
            flipped[r] = []
            for b in range(ROUND_BANKS):
                bank = flip_psum.tile([P, 2 * BANK_GROUPS, P], F32, tag="bank")
                for a in range(BANK_GROUPS):
                    for u in range(2):
                        if b >= FIRST_SORTED:
                            w0 = (2 * ((b - FIRST_SORTED) * BANK_GROUPS + a) + u) * P
                            run = sorted_tiles[r][:, w0 : w0 + P]
                        else:
                            w0 = (b * BANK_GROUPS + a) * 2 * P
                            run = x_words[:, w0 + u : w0 + 2 * P : 2]
                        nc.tensor.transpose(bank[:, 2 * a + u, :], run, identity[:])
                flipped[r].append(bank)

        def open_round(r):
            grouped = stage.tile([P, ROUND_COLS], BF16, align_bytes=64)
            codes = code_pool.tile([P, ROUND_GROUPS * P], U32, align_bytes=64)
            planes = code_pool.tile([P, ROUND_GROUPS * P], U8, align_bytes=64)
            grouped_tiles[r] = grouped
            code_tiles[r] = (codes, planes)

        def regroup_bank(r, b):
            dst = (
                grouped_tiles[r][:]
                .bitcast(F32)[:, b * BANK_WORDS : (b + 1) * BANK_WORDS]
                .rearrange("p (a r u) -> p a r u", a=BANK_GROUPS, u=2)
            )
            src = flipped[r][b][:].rearrange("p (a u) r -> p a r u", u=2)
            nc.scalar.copy(out=dst, in_=src)

        def quantise_banks(r, b0, n_banks):
            codes, planes = code_tiles[r]
            words = slice(b0 * BANK_COLS // PACK, (b0 + n_banks) * BANK_COLS // PACK)
            nc.vector.quantize_mx(
                out=codes[:, words].bitcast(FP8X4),
                scales=planes[:, words],
                in_=grouped_tiles[r][:, b0 * BANK_COLS : (b0 + n_banks) * BANK_COLS],
            )

        def multiply_banks(r, b0, n_banks):
            chunk, row_tile = divmod(r, ROW_TILES)
            codes, planes = code_tiles[r]
            for a in range(b0 * BANK_GROUPS, (b0 + n_banks) * BANK_GROUPS):
                g = chunk * ROUND_GROUPS + a
                rows = slice(a * P, (a + 1) * P)
                nc.tensor.matmul_mx(
                    out=acc[row_tile][:],
                    lhsT=codes[:, rows].bitcast(FP8X4),
                    lhsT_scale=planes[:, rows],
                    rhs=w_words[:, g, :].bitcast(FP4X4),
                    rhs_scale=w_planes[:, g, :],
                    start=(g == 0),
                    stop=(g == GROUPS - 1),
                )

        h_tiles = {}
        moment_tiles = {}
        std_tiles = {}

        def statistics(row_tile):
            h = keep.tile([P, FEATURES], F32, name="h%d" % row_tile)
            nc.vector.tensor_tensor(out=h[:], in0=acc[row_tile][:], in1=bias[:], op=ALU.add)
            stats = keep.tile([P, 6], F32, name="stats%d" % row_tile)
            nc.vector.bn_stats(out=stats[:], in_=h[:])
            moments = keep.tile([P, 2], F32, name="moments%d" % row_tile)
            nc.vector.bn_aggr(out=moments[:], in_=stats[:])
            std = keep.tile([P, 1], F32, name="std%d" % row_tile)
            nc.scalar.activation(
                out=std[:], in_=moments[:, 1:2], func=ACT.Abs_reciprocal_sqrt, bias=eps[:], scale=1.0
            )
            h_tiles[row_tile] = h
            moment_tiles[row_tile] = moments
            std_tiles[row_tile] = std

        def normalise(row_tile):
            inv_std = std_tiles[row_tile]
            normed = keep.tile([P, FEATURES], F32, name="normed%d" % row_tile)
            nc.vector.tensor_scalar(
                out=normed[:],
                in0=h_tiles[row_tile][:],
                scalar1=moment_tiles[row_tile][:, 0:1],
                scalar2=inv_std[:],
                op0=ALU.subtract,
                op1=ALU.mult,
            )
            result = keep.tile([P, FEATURES], F32, name="result%d" % row_tile)
            nc.vector.scalar_tensor_tensor(
                out=result[:], in0=normed[:], scalar=SLOPE, in1=normed[:], op0=ALU.mult, op1=ALU.max
            )
            nc.sync.dma_start(out=out_tiles[row_tile], in_=result[:])

        for c in range(SCALE_CUTS):
            nc.vector.memset(w_planes[:, c * CUT_GROUPS : (c + 1) * CUT_GROUPS, :].bitcast(I32), 0)
        nc.vector.memset(eps[:], EPS)
        nc.gpsimd.memset(bias_row[:], 0.0)
        nc.gpsimd.memset(ones[:], 1.0)
        make_identity(nc, identity[:])
        nc.scalar.dma_start(out=bias_row[0:1, :], in_=b1.unsqueeze(0))
        nc.scalar.activation(out=warm[:], in_=eps[:], func=ACT.Abs_reciprocal_sqrt)

        load_round(0)
        load_scales(0, nc.sync, I32)
        for c in range(1, SCALE_CUTS):
            load_scales(c, nc.gpsimd, F32)
        for r in range(1, X_BUFFERS):
            load_round(r)

        bias_bank = flip_psum.tile([P, 2 * BANK_GROUPS, P], F32, tag="bank")
        nc.tensor.matmul(out=bias_bank[:, 0, :], lhsT=ones[:], rhs=bias_row[:], start=True, stop=True)
        nc.vector.tensor_copy(out=bias[:], in_=bias_bank[:, 0, :])

        last = ROUNDS - 1
        sort_round(0)
        for r in range(ROUNDS):
            open_round(r)
            transpose_round(r)
            if r >= 1:
                quantise_banks(r - 1, HALF_BANKS, HALF_BANKS)
            if r < last:
                sort_round(r + 1)
            for b in range(ROUND_BANKS):
                regroup_bank(r, b)
                if b == HALF_BANKS - 1:
                    quantise_banks(r, 0, HALF_BANKS)
            if r + X_BUFFERS < ROUNDS:
                load_round(r + X_BUFFERS)
            if 1 <= r <= FIRST_LATE:
                multiply_banks(r - 1, 0, ROUND_BANKS)
        quantise_banks(last, HALF_BANKS, HALF_BANKS)

        for r in range(FIRST_LATE, ROUNDS):
            multiply_banks(r, 0, ROUND_BANKS)
            if r >= ROUNDS - ROW_TILES:
                statistics(r - (ROUNDS - ROW_TILES))
        normalise(0)
        normalise(1)
